import numpy as np
import ml_dtypes


def mxq(x, axis, fmt="e4m3"):
    dtype, down = {"e4m3": (ml_dtypes.float8_e4m3fn, 7), "e5m2": (ml_dtypes.float8_e5m2, 14)}[fmt]
    v = np.moveaxis(np.asarray(x, np.float32).astype(ml_dtypes.bfloat16).astype(np.float64), axis, -1)
    blocks = v.reshape(v.shape[:-1] + (-1, 32))
    amax = np.abs(blocks).max(-1, keepdims=True)
    byte = np.maximum(np.where(amax > 0, np.frexp(amax)[1] - 1 + 127, 0) - down, 1)
    scale = np.exp2(byte - 127.0)
    codes = (blocks / scale).astype(np.float32).astype(dtype).astype(np.float64)
    return np.moveaxis((codes * scale).reshape(v.shape), -1, axis)


WIDE = False


def mx_kscale(k):
    if not WIDE:
        return np.ones(k)
    levels = np.array([10, -10, 5, -5, 0])
    a = np.random.permutation(np.resize(levels, k // 512 * 4)).reshape(k // 512, 4)
    idx = np.arange(k)
    return np.exp2(a[idx // 512, idx % 128 // 32])


BF16 = ml_dtypes.bfloat16


def bf(x):
    return np.asarray(x, np.float32).astype(BF16)


def f64(x):
    return np.asarray(x).astype(np.float64)


E2M1 = np.array([0.0, 0.5, 1.0, 1.5, 2.0, 3.0, 4.0, 6.0, -0.0, -0.5, -1.0, -1.5, -2.0, -3.0, -4.0, -6.0])


def pack_weight(w, fmt):
    k, n = w.shape
    w = f64(bf(w)).reshape(k // 32, 32, n)
    amax = np.abs(w).max(1)
    if fmt == "e4m3":
        byte = np.frexp(amax)[1] - 1 + 127 - 7
    else:
        mant, ex = np.frexp(amax / 6.0)
        byte = np.where(mant > 0.5, ex, ex - 1) + 127
    byte = np.clip(np.where(amax > 0, byte, 1), 1, 254)
    scaled = (w * np.exp2(127.0 - byte)[:, None, :]).reshape(k, n).astype(np.float32)
    by_word = np.ascontiguousarray(scaled.reshape(k // 512, 128, 4, n).transpose(0, 1, 3, 2))
    if fmt == "e4m3":
        words = by_word.astype(ml_dtypes.float8_e4m3fn).view(np.uint8)
    else:
        c = by_word.astype(ml_dtypes.float4_e2m1fn).view(np.uint8) & 0xF
        words = c[..., 0::2] | (c[..., 1::2] << 4)
    return np.ascontiguousarray(words), np.ascontiguousarray(byte.astype(np.uint8).reshape(k // 512, 16, n))


def unpack_weight(words, scales, fmt):
    g, p, n, _ = words.shape
    if fmt == "e4m3":
        vals = np.ascontiguousarray(words).view(ml_dtypes.float8_e4m3fn).astype(np.float64)
    else:
        nib = np.empty((g, p, n, 4), np.uint8)
        nib[..., 0::2] = words & 0xF
        nib[..., 1::2] = words >> 4
        vals = E2M1[nib]
    vals = vals * np.repeat(np.exp2(scales.astype(np.float64) - 127.0), 8, axis=1)[..., None]
    return vals.transpose(0, 1, 3, 2).reshape(g * 512, n)


B, C, CI, N = 2, 1024, 512, 1024
EPS = 1e-5


def setup_inputs():
    s, t = mx_kscale(N), mx_kscale(CI)
    r = np.random.standard_normal
    affinity = bf(r((B, N, N)) * 0.2 * s[None, None, :])
    g_x = bf(r((B, N, CI)) / s[None, :, None] * t[None, None, :])
    w = r((C, CI)) * 1.5 / (0.2 * np.sqrt(N) * np.sqrt(CI)) / t[None, :]
    w_w_words, w_w_scales = pack_weight(np.ascontiguousarray(w.T), "e4m3")
    return {"affinity": affinity,
            "g_x": g_x,
            "w_w_words": w_w_words,
            "w_w_scales": w_w_scales,
            "w_b": bf(r(C) * 0.3),
            "bn_gamma": bf(r(C)),
            "bn_beta": bf(r(C) * 0.5),
            "bn_mean": bf(r(C) * 0.5),
            "bn_var": bf(np.random.uniform(0.5, 1.5, C)),
            "x": bf(r((B, C, N)))}


def reference(affinity, g_x, w_w_words, w_w_scales, w_b, bn_gamma, bn_beta, bn_mean, bn_var, x):
    y = (mxq(f64(affinity), 2, "e4m3") @ mxq(f64(g_x), 1, "e4m3")).transpose(0, 2, 1)
    wy = (unpack_weight(w_w_words, w_w_scales, "e4m3").T @ mxq(y, 1, "e4m3")) + f64(w_b)[None, :, None]
    inv_std = 1.0 / np.sqrt(f64(bn_var) + EPS)
    wy = f64(bn_gamma)[None, :, None] * (wy - f64(bn_mean)[None, :, None]) * inv_std[None, :, None] + f64(bn_beta)[None, :, None]
    return wy + f64(x)

@@ -1,0 +1,260 @@
+from contextlib import ExitStack
+
+import concourse.mybir as mybir
+from concourse.masks import make_identity
+
+F32 = mybir.dt.float32
+BF16 = mybir.dt.bfloat16
+I32 = mybir.dt.int32
+U32 = mybir.dt.uint32
+U8 = mybir.dt.uint8
+FP8X4 = mybir.dt.float8_e4m3fn_x4
+ALU = mybir.AluOpType
+ACT = mybir.ActivationFunctionType
+
+P = 128
+LANES = 4
+K_PASS = P * LANES
+BANK = 512
+
+BATCH = 2
+POINTS = 1024
+INNER = 512
+CHANNELS = 1024
+EPS = 1e-5
+
+PASSES = POINTS // K_PASS
+QBLOCK = 2 * P
+QUARTERS = POINTS // QBLOCK
+BLOCKS = BATCH * QUARTERS
+HALVES = POINTS // BANK
+CTILES = CHANNELS // P
+
+TURN_AHEAD = 1
+REGROUP_AHEAD = 2
+QUANTISE_AHEAD = 1
+PROJECT_LAG = QUARTERS
+SHIFT_LAG = PROJECT_LAG - 1
+GAIN_STEP = SHIFT_LAG - 2
+
+FLOPS = 2 * BATCH * (POINTS * POINTS * INNER + CHANNELS * INNER * POINTS)
+
+
+def tile_sgcam_pb_kernel(
+    tc, affinity, g_x, w_w_words, w_w_scales, w_b, bn_gamma, bn_beta, bn_mean, bn_var, x, out
+):
+    nc = tc.nc
+    with ExitStack() as ctx:
+        keep = ctx.enter_context(tc.tile_pool(name="keep", bufs=1))
+        stage = ctx.enter_context(tc.tile_pool(name="stage", bufs=3))
+        psum = ctx.enter_context(tc.psum_pool(name="psum", bufs=8))
+
+        identity = keep.tile([P, P], F32, name="identity")
+        make_identity(nc, identity[:])
+        minus_half = keep.tile([P, CTILES], F32, name="minus_half")
+        nc.gpsimd.memset(minus_half[:], -0.5)
+        w_scales = keep.tile([P, CHANNELS], U8, name="w_scales", align_bytes=64)
+        nc.vector.memset(w_scales[:].bitcast(I32), 0)
+        vector_rows = keep.tile([P, P], BF16, name="vector_rows")
+        nc.vector.memset(vector_rows[:], 0.0)
+        warm = keep.tile([P, 1], F32, name="warm")
+        nc.vector.memset(warm[:], 0.0)
+        nc.scalar.activation(out=warm[:], in_=warm[:], func=ACT.Identity)
+
+        for v, vector in enumerate((w_b, bn_gamma, bn_beta, bn_mean, bn_var)):
+            nc.scalar.dma_start(
+                out=vector_rows[CTILES * v : CTILES * (v + 1), :], in_=vector.rearrange("(i p) -> i p", p=P)
+            )
+        g_raw = []
+        a_raw = []
+        x_raw = []
+        w_codes = keep.tile([P, CHANNELS], U32, name="w_codes", align_bytes=64)
+        for n in range(BLOCKS + PROJECT_LAG):
+            if n < BLOCKS:
+                b, quarter = divmod(n, QUARTERS)
+                if quarter == 0:
+                    g_raw.append(keep.tile([P, PASSES, LANES, INNER], BF16, name="g_raw%d" % b))
+                    for g in range(PASSES):
+                        nc.sync.dma_start(
+                            out=g_raw[b][:, g].rearrange("j (u e) c -> j u (e c)", u=2),
+                            in_=g_x[b, g * K_PASS : (g + 1) * K_PASS, :].rearrange(
+                                "(u j e) c -> j u (e c)", u=2, e=2
+                            ),
+                        )
+                a_raw.append(keep.tile([P, 2, POINTS], BF16, name="a_raw%d" % n))
+                nc.sync.dma_start(
+                    out=a_raw[n][:],
+                    in_=affinity[b, quarter * QBLOCK : (quarter + 1) * QBLOCK, :].rearrange("(p r) s -> p r s", r=2),
+                )
+                if b == 0:
+                    nc.sync.dma_start(
+                        out=w_scales[32 * quarter : 32 * quarter + LANES, :].bitcast(I32),
+                        in_=w_w_scales[0, LANES * quarter : LANES * (quarter + 1), :].bitcast(I32),
+                    )
+            if n == PROJECT_LAG:
+                nc.sync.dma_start(
+                    out=w_codes[:].bitcast(I32), in_=w_w_words[0].rearrange("p n t -> p (n t)").bitcast(I32)
+                )
+            if n >= PROJECT_LAG:
+                b, quarter = divmod(n - PROJECT_LAG, QUARTERS)
+                x_raw.append(keep.tile([P, 2, POINTS], BF16, name="x_raw%d" % (n - PROJECT_LAG)))
+                nc.sync.dma_start(
+                    out=x_raw[-1][:],
+                    in_=x[b, quarter * 2 * P : (quarter + 1) * 2 * P, :].rearrange("(i p) q -> p i q", p=P),
+                )
+
+        vector_rows_f32 = keep.tile([P, P], F32, name="vector_rows_f32")
+        nc.gpsimd.tensor_copy(out=vector_rows_f32[:], in_=vector_rows[:])
+        gain = keep.tile([P, CTILES], F32, name="gain")
+        shift = keep.tile([P, CTILES], F32, name="shift")
+
+        g_grouped = {}
+        g_quantised = {}
+        a_grouped = {}
+        y_grouped = {}
+        y_quantised = {}
+        results = {}
+
+        def regroup_values(b):
+            g_grouped[b] = stage.tile([P, PASSES, INNER * LANES], BF16, name="g_grouped", bufs=1, align_bytes=64)
+            for g in range(PASSES):
+                nc.vector.tensor_copy(
+                    out=g_grouped[b][:, g, :].rearrange("j (l m s) -> j l m s", l=LANES, s=LANES),
+                    in_=g_raw[b][:, g].rearrange("j s (m l) -> j l m s", l=LANES),
+                )
+
+        def quantise_values(b):
+            g_codes = keep.tile([P, PASSES * INNER], U32, name="g_codes%d" % b, align_bytes=64)
+            g_scales = keep.tile([P, PASSES * INNER], U8, name="g_scales%d" % b, align_bytes=64)
+            nc.vector.quantize_mx(
+                out=g_codes[:].bitcast(FP8X4), scales=g_scales[:], in_=g_grouped[b][:].rearrange("j g c -> j (g c)")
+            )
+            g_quantised[b] = (g_codes, g_scales)
+
+        def transpose_block(n):
+            words = a_raw[n][:].bitcast(F32)
+            a_grouped[n] = stage.tile([P, PASSES, QBLOCK * LANES], BF16, name="a_grouped", align_bytes=64)
+            for g in range(PASSES):
+                turned = psum.tile([P, 2, 2, P], F32, name="turned", tag="bank")
+                for r in range(2):
+                    for u in range(2):
+                        first = (g * 2 + u) * P
+                        nc.tensor.transpose(turned[:, r, u, :], words[:, r, first : first + P], identity[:])
+                nc.scalar.copy(
+                    out=a_grouped[n][:, g, :].bitcast(F32).rearrange("j (p r u) -> j p r u", r=2, u=2),
+                    in_=turned[:].rearrange("j r u p -> j p r u"),
+                )
+
+        def first_product(n):
+            b, quarter = divmod(n, QUARTERS)
+            half, part = divmod(quarter, QUARTERS // HALVES)
+            a_codes = stage.tile([P, PASSES * QBLOCK], U32, name="a_codes", align_bytes=64)
+            a_scales = stage.tile([P, PASSES * QBLOCK], U8, name="a_scales", align_bytes=64)
+            nc.vector.quantize_mx(
+                out=a_codes[:].bitcast(FP8X4), scales=a_scales[:], in_=a_grouped[n][:].rearrange("j g c -> j (g c)")
+            )
+            if quarter == QUARTERS - QUANTISE_AHEAD and b + 1 < BATCH:
+                quantise_values(b + 1)
+            g_codes, g_scales = g_quantised[b]
+            if part == 0:
+                y_grouped[b, half] = stage.tile([P, BANK, LANES], BF16, name="y_grouped", align_bytes=64)
+            for k in range(QBLOCK // P):
+                sums = psum.tile([P, LANES, P], F32, name="sums", tag="bank")
+                for l in range(LANES):
+                    for g in range(PASSES):
+                        stationary = slice(g * INNER + l * P, g * INNER + (l + 1) * P)
+                        moving = slice(g * QBLOCK + k * P, g * QBLOCK + (k + 1) * P)
+                        nc.tensor.matmul_mx(
+                            out=sums[:, l, :],
+                            lhsT=g_codes[:, stationary].bitcast(FP8X4),
+                            lhsT_scale=g_scales[:, stationary],
+                            rhs=a_codes[:, moving].bitcast(FP8X4),
+                            rhs_scale=a_scales[:, moving],
+                            start=(g == 0),
+                            stop=(g == PASSES - 1),
+                        )
+                first = part * QBLOCK + k * P
+                nc.scalar.copy(out=y_grouped[b, half][:, first : first + P, :], in_=sums[:].rearrange("m l q -> m q l"))
+            if part == QUARTERS // HALVES - 1:
+                y_codes = keep.tile([P, BANK], U32, name="y_codes%d_%d" % (b, half), align_bytes=64)
+                y_scales = keep.tile([P, BANK], U8, name="y_scales%d_%d" % (b, half), align_bytes=64)
+                nc.vector.quantize_mx(
+                    out=y_codes[:].bitcast(FP8X4),
+                    scales=y_scales[:],
+                    in_=y_grouped[b, half][:].rearrange("m q l -> m (q l)"),
+                )
+                y_quantised[b, half] = (y_codes, y_scales)
+
+        def make_gain_and_shift():
+            turned_vectors = psum.tile([P, BANK], F32, name="turned_vectors", tag="bank")
+            nc.tensor.transpose(turned_vectors[:, 0:P], vector_rows_f32[:], identity[:])
+            per_channel = keep.tile([P, 5, CTILES], F32, name="per_channel")
+            nc.scalar.copy(out=per_channel[:].rearrange("p v i -> p (v i)"), in_=turned_vectors[:, 0 : 5 * CTILES])
+            bias_c, gamma_c, beta_c, mean_c, var_c = [per_channel[:, v, :] for v in range(5)]
+            nc.gpsimd.tensor_scalar(out=gain[:], in0=var_c, scalar1=1.0, scalar2=EPS, op0=ALU.mult, op1=ALU.add)
+            nc.gpsimd.tensor_tensor(out=gain[:], in0=gain[:], in1=minus_half[:], op=ALU.pow)
+            nc.gpsimd.tensor_tensor(out=gain[:], in0=gain[:], in1=gamma_c, op=ALU.mult)
+            nc.gpsimd.tensor_tensor(out=shift[:], in0=bias_c, in1=mean_c, op=ALU.subtract)
+            nc.gpsimd.tensor_tensor(out=shift[:], in0=shift[:], in1=gain[:], op=ALU.mult)
+            nc.gpsimd.tensor_tensor(out=shift[:], in0=shift[:], in1=beta_c, op=ALU.add)
+
+        def add_shift(n):
+            b, quarter = divmod(n, QUARTERS)
+            even, odd = 2 * quarter, 2 * quarter + 1
+            results[b, even] = keep.tile([P, POINTS], F32, name="result%d_%d" % (b, even))
+            results[b, odd] = keep.tile([P, POINTS], F32, name="result%d_%d" % (b, odd))
+            nc.scalar.activation(
+                out=results[b, even][:], in_=x_raw[n][:, 0, :], func=ACT.Identity, bias=shift[:, even : even + 1]
+            )
+            nc.gpsimd.tensor_scalar(
+                out=results[b, odd][:],
+                in0=x_raw[n][:, 1, :],
+                scalar1=1.0,
+                scalar2=shift[:, odd : odd + 1],
+                op0=ALU.mult,
+                op1=ALU.add,
+            )
+
+        def second_product(n):
+            b, quarter = divmod(n, QUARTERS)
+            for i in (2 * quarter, 2 * quarter + 1):
+                channels = slice(i * P, (i + 1) * P)
+                for half in range(HALVES):
+                    points = slice(half * BANK, (half + 1) * BANK)
+                    y_codes, y_scales = y_quantised[b, half]
+                    projected = psum.tile([P, BANK], F32, name="projected", tag="bank")
+                    nc.tensor.matmul_mx(
+                        out=projected[:],
+                        lhsT=w_codes[:, channels].bitcast(FP8X4),
+                        lhsT_scale=w_scales[:, channels],
+                        rhs=y_codes[:].bitcast(FP8X4),
+                        rhs_scale=y_scales[:],
+                        start=True,
+                        stop=True,
+                    )
+                    nc.vector.scalar_tensor_tensor(
+                        out=results[b, i][:, points],
+                        in0=projected[:],
+                        scalar=gain[:, i : i + 1],
+                        in1=results[b, i][:, points],
+                        op0=ALU.mult,
+                        op1=ALU.add,
+                    )
+                nc.sync.dma_start(out=out[b, channels, :], in_=results[b, i][:])
+
+        regroup_values(0)
+        quantise_values(0)
+        transpose_block(0)
+        for step in range(BLOCKS + PROJECT_LAG):
+            if step + TURN_AHEAD < BLOCKS:
+                transpose_block(step + TURN_AHEAD)
+            if step < BLOCKS:
+                first_product(step)
+            if (step + REGROUP_AHEAD) % QUARTERS == 0 and step + REGROUP_AHEAD < BLOCKS:
+                regroup_values((step + REGROUP_AHEAD) // QUARTERS)
+            if step == GAIN_STEP:
+                make_gain_and_shift()
+            if 0 <= step - SHIFT_LAG < BLOCKS:
+                add_shift(step - SHIFT_LAG)
+            if 0 <= step - PROJECT_LAG:
+                second_product(step - PROJECT_LAG)

@@ -28,11 +28,13 @@ QBLOCK = 2 * P
 QUARTERS = POINTS // QBLOCK
 BLOCKS = BATCH * QUARTERS
 HALVES = POINTS // BANK
+BLOCKS_PER_BANK = BANK // QBLOCK
 CTILES = CHANNELS // P
 
-TURN_AHEAD = 1
-REGROUP_AHEAD = 2
+REGROUP_AHEAD = 3
 QUANTISE_AHEAD = 1
+TURN_AHEAD = 1
+Y_LAG = 1
 PROJECT_LAG = QUARTERS
 SHIFT_LAG = PROJECT_LAG - 1
 GAIN_STEP = SHIFT_LAG - 2
@@ -48,6 +50,7 @@ def tile_sgcam_pb_kernel(
         keep = ctx.enter_context(tc.tile_pool(name="keep", bufs=1))
         stage = ctx.enter_context(tc.tile_pool(name="stage", bufs=3))
         psum = ctx.enter_context(tc.psum_pool(name="psum", bufs=8))
+        ctx.enter_context(tc.manual_schedule())
 
         identity = keep.tile([P, P], F32, name="identity")
         make_identity(nc, identity[:])
@@ -111,17 +114,18 @@ def tile_sgcam_pb_kernel(
         g_grouped = {}
         g_quantised = {}
         a_grouped = {}
+        a_quantised = {}
         y_grouped = {}
         y_quantised = {}
         results = {}
 
-        def regroup_values(b):
-            g_grouped[b] = stage.tile([P, PASSES, INNER * LANES], BF16, name="g_grouped", bufs=1, align_bytes=64)
-            for g in range(PASSES):
-                nc.vector.tensor_copy(
-                    out=g_grouped[b][:, g, :].rearrange("j (l m s) -> j l m s", l=LANES, s=LANES),
-                    in_=g_raw[b][:, g].rearrange("j s (m l) -> j l m s", l=LANES),
-                )
+        def regroup_values(b, g):
+            if g == 0:
+                g_grouped[b] = stage.tile([P, PASSES, INNER * LANES], BF16, name="g_grouped", bufs=1, align_bytes=64)
+            nc.vector.tensor_copy(
+                out=g_grouped[b][:, g, :].rearrange("j (l m s) -> j l m s", l=LANES, s=LANES),
+                in_=g_raw[b][:, g].rearrange("j s (m l) -> j l m s", l=LANES),
+            )
 
         def quantise_values(b):
             g_codes = keep.tile([P, PASSES * INNER], U32, name="g_codes%d" % b, align_bytes=64)
@@ -145,16 +149,18 @@ def tile_sgcam_pb_kernel(
                     in_=turned[:].rearrange("j r u p -> j p r u"),
                 )
 
-        def first_product(n):
-            b, quarter = divmod(n, QUARTERS)
-            half, part = divmod(quarter, QUARTERS // HALVES)
+        def quantise_block(n):
             a_codes = stage.tile([P, PASSES * QBLOCK], U32, name="a_codes", align_bytes=64)
             a_scales = stage.tile([P, PASSES * QBLOCK], U8, name="a_scales", align_bytes=64)
             nc.vector.quantize_mx(
                 out=a_codes[:].bitcast(FP8X4), scales=a_scales[:], in_=a_grouped[n][:].rearrange("j g c -> j (g c)")
             )
-            if quarter == QUARTERS - QUANTISE_AHEAD and b + 1 < BATCH:
-                quantise_values(b + 1)
+            a_quantised[n] = (a_codes, a_scales)
+
+        def first_product(n):
+            b, quarter = divmod(n, QUARTERS)
+            half, part = divmod(quarter, BLOCKS_PER_BANK)
+            a_codes, a_scales = a_quantised[n]
             g_codes, g_scales = g_quantised[b]
             if part == 0:
                 y_grouped[b, half] = stage.tile([P, BANK, LANES], BF16, name="y_grouped", align_bytes=64)
@@ -175,7 +181,11 @@ def tile_sgcam_pb_kernel(
                         )
                 first = part * QBLOCK + k * P
                 nc.scalar.copy(out=y_grouped[b, half][:, first : first + P, :], in_=sums[:].rearrange("m l q -> m q l"))
-            if part == QUARTERS // HALVES - 1:
+
+        def quantise_y(n):
+            b, quarter = divmod(n, QUARTERS)
+            half, part = divmod(quarter, BLOCKS_PER_BANK)
+            if part == BLOCKS_PER_BANK - 1:
                 y_codes = keep.tile([P, BANK], U32, name="y_codes%d_%d" % (b, half), align_bytes=64)
                 y_scales = keep.tile([P, BANK], U8, name="y_scales%d_%d" % (b, half), align_bytes=64)
                 nc.vector.quantize_mx(
@@ -242,19 +252,30 @@ def tile_sgcam_pb_kernel(
                     )
                 nc.sync.dma_start(out=out[b, channels, :], in_=results[b, i][:])
 
-        regroup_values(0)
-        quantise_values(0)
-        transpose_block(0)
-        for step in range(BLOCKS + PROJECT_LAG):
-            if step + TURN_AHEAD < BLOCKS:
+        def is_block(n):
+            return 0 <= n < BLOCKS
+
+        def batch_that_starts(step):
+            b, quarter = divmod(step, QUARTERS)
+            return b if quarter == 0 and 0 <= b < BATCH else None
+
+        for step in range(-REGROUP_AHEAD, BLOCKS + PROJECT_LAG):
+            if is_block(step + TURN_AHEAD):
                 transpose_block(step + TURN_AHEAD)
-            if step < BLOCKS:
+            if is_block(step - SHIFT_LAG):
+                add_shift(step - SHIFT_LAG)
+            if is_block(step):
+                quantise_block(step)
+            if is_block(step - Y_LAG):
+                quantise_y(step - Y_LAG)
+            if batch_that_starts(step + QUANTISE_AHEAD) is not None:
+                quantise_values(batch_that_starts(step + QUANTISE_AHEAD))
+            if is_block(step - PROJECT_LAG):
+                second_product(step - PROJECT_LAG)
+            if is_block(step):
                 first_product(step)
-            if (step + REGROUP_AHEAD) % QUARTERS == 0 and step + REGROUP_AHEAD < BLOCKS:
-                regroup_values((step + REGROUP_AHEAD) // QUARTERS)
+            for g in range(PASSES):
+                if batch_that_starts(step + REGROUP_AHEAD - g) is not None:
+                    regroup_values(batch_that_starts(step + REGROUP_AHEAD - g), g)
             if step == GAIN_STEP:
                 make_gain_and_shift()
-            if 0 <= step - SHIFT_LAG < BLOCKS:
-                add_shift(step - SHIFT_LAG)
-            if 0 <= step - PROJECT_LAG:
-                second_product(step - PROJECT_LAG)

@@ -13,9 +13,14 @@ ALU = mybir.AluOpType
 ACT = mybir.ActivationFunctionType
 
 P = 128
+QUADRANT = 32
 LANES = 4
+WORD = 2
+SPANS = LANES // WORD
+ALIGN = 64
 K_PASS = P * LANES
 BANK = 512
+BANKS = 8
 
 BATCH = 2
 POINTS = 1024
@@ -24,17 +29,19 @@ CHANNELS = 1024
 EPS = 1e-5
 
 PASSES = POINTS // K_PASS
-QBLOCK = 2 * P
+ROWS = 2
+QBLOCK = ROWS * P
 QUARTERS = POINTS // QBLOCK
 BLOCKS = BATCH * QUARTERS
 HALVES = POINTS // BANK
-BLOCKS_PER_BANK = BANK // QBLOCK
+BLOCKS_PER_HALF = BANK // QBLOCK
 CTILES = CHANNELS // P
+PAIR = CTILES // QUARTERS
+VECTORS = 5
 
-REGROUP_AHEAD = 3
-QUANTISE_AHEAD = 1
 TURN_AHEAD = 1
-Y_LAG = 1
+REGROUP_AHEAD = 2
+QUANTISE_AHEAD = 1
 PROJECT_LAG = QUARTERS
 SHIFT_LAG = PROJECT_LAG - 1
 GAIN_STEP = SHIFT_LAG - 2
@@ -49,14 +56,13 @@ def tile_sgcam_pb_kernel(
     with ExitStack() as ctx:
         keep = ctx.enter_context(tc.tile_pool(name="keep", bufs=1))
         stage = ctx.enter_context(tc.tile_pool(name="stage", bufs=3))
-        psum = ctx.enter_context(tc.psum_pool(name="psum", bufs=8))
-        ctx.enter_context(tc.manual_schedule())
+        psum = ctx.enter_context(tc.psum_pool(name="psum", bufs=BANKS))
 
         identity = keep.tile([P, P], F32, name="identity")
         make_identity(nc, identity[:])
         minus_half = keep.tile([P, CTILES], F32, name="minus_half")
         nc.gpsimd.memset(minus_half[:], -0.5)
-        w_scales = keep.tile([P, CHANNELS], U8, name="w_scales", align_bytes=64)
+        w_scales = keep.tile([P, CHANNELS], U8, name="w_scales", align_bytes=ALIGN)
         nc.vector.memset(w_scales[:].bitcast(I32), 0)
         vector_rows = keep.tile([P, P], BF16, name="vector_rows")
         nc.vector.memset(vector_rows[:], 0.0)
@@ -71,7 +77,7 @@ def tile_sgcam_pb_kernel(
         g_raw = []
         a_raw = []
         x_raw = []
-        w_codes = keep.tile([P, CHANNELS], U32, name="w_codes", align_bytes=64)
+        w_codes = keep.tile([P, CHANNELS], U32, name="w_codes", align_bytes=ALIGN)
         for n in range(BLOCKS + PROJECT_LAG):
             if n < BLOCKS:
                 b, quarter = divmod(n, QUARTERS)
@@ -79,19 +85,21 @@ def tile_sgcam_pb_kernel(
                     g_raw.append(keep.tile([P, PASSES, LANES, INNER], BF16, name="g_raw%d" % b))
                     for g in range(PASSES):
                         nc.sync.dma_start(
-                            out=g_raw[b][:, g].rearrange("j (u e) c -> j u (e c)", u=2),
+                            out=g_raw[b][:, g].rearrange("j (u e) c -> j u (e c)", u=SPANS),
                             in_=g_x[b, g * K_PASS : (g + 1) * K_PASS, :].rearrange(
-                                "(u j e) c -> j u (e c)", u=2, e=2
+                                "(u j e) c -> j u (e c)", u=SPANS, e=WORD
                             ),
                         )
-                a_raw.append(keep.tile([P, 2, POINTS], BF16, name="a_raw%d" % n))
+                a_raw.append(keep.tile([P, ROWS, POINTS], BF16, name="a_raw%d" % n))
                 nc.sync.dma_start(
                     out=a_raw[n][:],
-                    in_=affinity[b, quarter * QBLOCK : (quarter + 1) * QBLOCK, :].rearrange("(p r) s -> p r s", r=2),
+                    in_=affinity[b, quarter * QBLOCK : (quarter + 1) * QBLOCK, :].rearrange(
+                        "(p r) s -> p r s", r=ROWS
+                    ),
                 )
                 if b == 0:
                     nc.sync.dma_start(
-                        out=w_scales[32 * quarter : 32 * quarter + LANES, :].bitcast(I32),
+                        out=w_scales[QUADRANT * quarter : QUADRANT * quarter + LANES, :].bitcast(I32),
                         in_=w_w_scales[0, LANES * quarter : LANES * (quarter + 1), :].bitcast(I32),
                     )
             if n == PROJECT_LAG:
@@ -100,10 +108,10 @@ def tile_sgcam_pb_kernel(
                 )
             if n >= PROJECT_LAG:
                 b, quarter = divmod(n - PROJECT_LAG, QUARTERS)
-                x_raw.append(keep.tile([P, 2, POINTS], BF16, name="x_raw%d" % (n - PROJECT_LAG)))
+                x_raw.append(keep.tile([P, PAIR, POINTS], BF16, name="x_raw%d" % (n - PROJECT_LAG)))
                 nc.sync.dma_start(
                     out=x_raw[-1][:],
-                    in_=x[b, quarter * 2 * P : (quarter + 1) * 2 * P, :].rearrange("(i p) q -> p i q", p=P),
+                    in_=x[b, quarter * PAIR * P : (quarter + 1) * PAIR * P, :].rearrange("(i p) q -> p i q", p=P),
                 )
 
         vector_rows_f32 = keep.tile([P, P], F32, name="vector_rows_f32")
@@ -119,17 +127,17 @@ def tile_sgcam_pb_kernel(
         y_quantised = {}
         results = {}
 
-        def regroup_values(b, g):
-            if g == 0:
-                g_grouped[b] = stage.tile([P, PASSES, INNER * LANES], BF16, name="g_grouped", bufs=1, align_bytes=64)
-            nc.vector.tensor_copy(
-                out=g_grouped[b][:, g, :].rearrange("j (l m s) -> j l m s", l=LANES, s=LANES),
-                in_=g_raw[b][:, g].rearrange("j s (m l) -> j l m s", l=LANES),
-            )
+        def regroup_values(b):
+            g_grouped[b] = stage.tile([P, PASSES, INNER * LANES], BF16, name="g_grouped", bufs=1, align_bytes=ALIGN)
+            for g in range(PASSES):
+                nc.vector.tensor_copy(
+                    out=g_grouped[b][:, g, :].rearrange("j (l m t) -> j l m t", l=LANES, t=LANES),
+                    in_=g_raw[b][:, g].rearrange("j t (m l) -> j l m t", l=LANES),
+                )
 
         def quantise_values(b):
-            g_codes = keep.tile([P, PASSES * INNER], U32, name="g_codes%d" % b, align_bytes=64)
-            g_scales = keep.tile([P, PASSES * INNER], U8, name="g_scales%d" % b, align_bytes=64)
+            g_codes = keep.tile([P, PASSES * INNER], U32, name="g_codes%d" % b, align_bytes=ALIGN)
+            g_scales = keep.tile([P, PASSES * INNER], U8, name="g_scales%d" % b, align_bytes=ALIGN)
             nc.vector.quantize_mx(
                 out=g_codes[:].bitcast(FP8X4), scales=g_scales[:], in_=g_grouped[b][:].rearrange("j g c -> j (g c)")
             )
@@ -137,21 +145,21 @@ def tile_sgcam_pb_kernel(
 
         def transpose_block(n):
             words = a_raw[n][:].bitcast(F32)
-            a_grouped[n] = stage.tile([P, PASSES, QBLOCK * LANES], BF16, name="a_grouped", align_bytes=64)
+            a_grouped[n] = stage.tile([P, PASSES, QBLOCK * LANES], BF16, name="a_grouped", align_bytes=ALIGN)
             for g in range(PASSES):
-                turned = psum.tile([P, 2, 2, P], F32, name="turned", tag="bank")
-                for r in range(2):
-                    for u in range(2):
-                        first = (g * 2 + u) * P
-                        nc.tensor.transpose(turned[:, r, u, :], words[:, r, first : first + P], identity[:])
+                turned = psum.tile([P, ROWS, SPANS, P], F32, name="turned", tag="bank")
+                for r in range(ROWS):
+                    for u in range(SPANS):
+                        first_word = (g * SPANS + u) * P
+                        nc.tensor.transpose(turned[:, r, u, :], words[:, r, first_word : first_word + P], identity[:])
                 nc.scalar.copy(
-                    out=a_grouped[n][:, g, :].bitcast(F32).rearrange("j (p r u) -> j p r u", r=2, u=2),
+                    out=a_grouped[n][:, g, :].bitcast(F32).rearrange("j (p r u) -> j p r u", r=ROWS, u=SPANS),
                     in_=turned[:].rearrange("j r u p -> j p r u"),
                 )
 
         def quantise_block(n):
-            a_codes = stage.tile([P, PASSES * QBLOCK], U32, name="a_codes", align_bytes=64)
-            a_scales = stage.tile([P, PASSES * QBLOCK], U8, name="a_scales", align_bytes=64)
+            a_codes = stage.tile([P, PASSES * QBLOCK], U32, name="a_codes", align_bytes=ALIGN)
+            a_scales = stage.tile([P, PASSES * QBLOCK], U8, name="a_scales", align_bytes=ALIGN)
             nc.vector.quantize_mx(
                 out=a_codes[:].bitcast(FP8X4), scales=a_scales[:], in_=a_grouped[n][:].rearrange("j g c -> j (g c)")
             )
@@ -159,17 +167,17 @@ def tile_sgcam_pb_kernel(
 
         def first_product(n):
             b, quarter = divmod(n, QUARTERS)
-            half, part = divmod(quarter, BLOCKS_PER_BANK)
+            half, part = divmod(quarter, BLOCKS_PER_HALF)
             a_codes, a_scales = a_quantised[n]
             g_codes, g_scales = g_quantised[b]
             if part == 0:
-                y_grouped[b, half] = stage.tile([P, BANK, LANES], BF16, name="y_grouped", align_bytes=64)
-            for k in range(QBLOCK // P):
+                y_grouped[b, half] = stage.tile([P, BANK, LANES], BF16, name="y_grouped", align_bytes=ALIGN)
+            for sub in range(QBLOCK // P):
                 sums = psum.tile([P, LANES, P], F32, name="sums", tag="bank")
                 for l in range(LANES):
                     for g in range(PASSES):
                         stationary = slice(g * INNER + l * P, g * INNER + (l + 1) * P)
-                        moving = slice(g * QBLOCK + k * P, g * QBLOCK + (k + 1) * P)
+                        moving = slice(g * QBLOCK + sub * P, g * QBLOCK + (sub + 1) * P)
                         nc.tensor.matmul_mx(
                             out=sums[:, l, :],
                             lhsT=g_codes[:, stationary].bitcast(FP8X4),
@@ -179,15 +187,13 @@ def tile_sgcam_pb_kernel(
                             start=(g == 0),
                             stop=(g == PASSES - 1),
                         )
-                first = part * QBLOCK + k * P
-                nc.scalar.copy(out=y_grouped[b, half][:, first : first + P, :], in_=sums[:].rearrange("m l q -> m q l"))
-
-        def quantise_y(n):
-            b, quarter = divmod(n, QUARTERS)
-            half, part = divmod(quarter, BLOCKS_PER_BANK)
-            if part == BLOCKS_PER_BANK - 1:
-                y_codes = keep.tile([P, BANK], U32, name="y_codes%d_%d" % (b, half), align_bytes=64)
-                y_scales = keep.tile([P, BANK], U8, name="y_scales%d_%d" % (b, half), align_bytes=64)
+                first_point = part * QBLOCK + sub * P
+                nc.scalar.copy(
+                    out=y_grouped[b, half][:, first_point : first_point + P, :], in_=sums[:].rearrange("m l q -> m q l")
+                )
+            if part == BLOCKS_PER_HALF - 1:
+                y_codes = keep.tile([P, BANK], U32, name="y_codes%d_%d" % (b, half), align_bytes=ALIGN)
+                y_scales = keep.tile([P, BANK], U8, name="y_scales%d_%d" % (b, half), align_bytes=ALIGN)
                 nc.vector.quantize_mx(
                     out=y_codes[:].bitcast(FP8X4),
                     scales=y_scales[:],
@@ -198,9 +204,11 @@ def tile_sgcam_pb_kernel(
         def make_gain_and_shift():
             turned_vectors = psum.tile([P, BANK], F32, name="turned_vectors", tag="bank")
             nc.tensor.transpose(turned_vectors[:, 0:P], vector_rows_f32[:], identity[:])
-            per_channel = keep.tile([P, 5, CTILES], F32, name="per_channel")
-            nc.scalar.copy(out=per_channel[:].rearrange("p v i -> p (v i)"), in_=turned_vectors[:, 0 : 5 * CTILES])
-            bias_c, gamma_c, beta_c, mean_c, var_c = [per_channel[:, v, :] for v in range(5)]
+            per_channel = keep.tile([P, VECTORS, CTILES], F32, name="per_channel")
+            nc.scalar.copy(
+                out=per_channel[:].rearrange("p v i -> p (v i)"), in_=turned_vectors[:, 0 : VECTORS * CTILES]
+            )
+            bias_c, gamma_c, beta_c, mean_c, var_c = [per_channel[:, v, :] for v in range(VECTORS)]
             nc.gpsimd.tensor_scalar(out=gain[:], in0=var_c, scalar1=1.0, scalar2=EPS, op0=ALU.mult, op1=ALU.add)
             nc.gpsimd.tensor_tensor(out=gain[:], in0=gain[:], in1=minus_half[:], op=ALU.pow)
             nc.gpsimd.tensor_tensor(out=gain[:], in0=gain[:], in1=gamma_c, op=ALU.mult)
@@ -210,24 +218,17 @@ def tile_sgcam_pb_kernel(
 
         def add_shift(n):
             b, quarter = divmod(n, QUARTERS)
-            even, odd = 2 * quarter, 2 * quarter + 1
+            even, odd = PAIR * quarter, PAIR * quarter + 1
             results[b, even] = keep.tile([P, POINTS], F32, name="result%d_%d" % (b, even))
             results[b, odd] = keep.tile([P, POINTS], F32, name="result%d_%d" % (b, odd))
             nc.scalar.activation(
                 out=results[b, even][:], in_=x_raw[n][:, 0, :], func=ACT.Identity, bias=shift[:, even : even + 1]
             )
-            nc.gpsimd.tensor_scalar(
-                out=results[b, odd][:],
-                in0=x_raw[n][:, 1, :],
-                scalar1=1.0,
-                scalar2=shift[:, odd : odd + 1],
-                op0=ALU.mult,
-                op1=ALU.add,
-            )
+            nc.vector.tensor_scalar_add(out=results[b, odd][:], in0=x_raw[n][:, 1, :], scalar1=shift[:, odd : odd + 1])
 
         def second_product(n):
             b, quarter = divmod(n, QUARTERS)
-            for i in (2 * quarter, 2 * quarter + 1):
+            for i in (PAIR * quarter, PAIR * quarter + 1):
                 channels = slice(i * P, (i + 1) * P)
                 for half in range(HALVES):
                     points = slice(half * BANK, (half + 1) * BANK)
@@ -255,27 +256,27 @@ def tile_sgcam_pb_kernel(
         def is_block(n):
             return 0 <= n < BLOCKS
 
-        def batch_that_starts(step):
+        def later_batch_that_starts(step):
             b, quarter = divmod(step, QUARTERS)
-            return b if quarter == 0 and 0 <= b < BATCH else None
+            return b if quarter == 0 and 0 < b < BATCH else None
 
-        for step in range(-REGROUP_AHEAD, BLOCKS + PROJECT_LAG):
+        regroup_values(0)
+        quantise_values(0)
+        transpose_block(0)
+        for step in range(BLOCKS + PROJECT_LAG):
             if is_block(step + TURN_AHEAD):
                 transpose_block(step + TURN_AHEAD)
-            if is_block(step - SHIFT_LAG):
-                add_shift(step - SHIFT_LAG)
             if is_block(step):
                 quantise_block(step)
-            if is_block(step - Y_LAG):
-                quantise_y(step - Y_LAG)
-            if batch_that_starts(step + QUANTISE_AHEAD) is not None:
-                quantise_values(batch_that_starts(step + QUANTISE_AHEAD))
-            if is_block(step - PROJECT_LAG):
-                second_product(step - PROJECT_LAG)
+            if later_batch_that_starts(step + QUANTISE_AHEAD) is not None:
+                quantise_values(later_batch_that_starts(step + QUANTISE_AHEAD))
             if is_block(step):
                 first_product(step)
-            for g in range(PASSES):
-                if batch_that_starts(step + REGROUP_AHEAD - g) is not None:
-                    regroup_values(batch_that_starts(step + REGROUP_AHEAD - g), g)
+            if later_batch_that_starts(step + REGROUP_AHEAD) is not None:
+                regroup_values(later_batch_that_starts(step + REGROUP_AHEAD))
             if step == GAIN_STEP:
                 make_gain_and_shift()
+            if is_block(step - SHIFT_LAG):
+                add_shift(step - SHIFT_LAG)
+            if is_block(step - PROJECT_LAG):
+                second_product(step - PROJECT_LAG)

from contextlib import ExitStack

import concourse.mybir as mybir
from concourse.masks import make_identity

F32 = mybir.dt.float32
BF16 = mybir.dt.bfloat16
I32 = mybir.dt.int32
U32 = mybir.dt.uint32
U8 = mybir.dt.uint8
FP8X4 = mybir.dt.float8_e4m3fn_x4
ALU = mybir.AluOpType
ACT = mybir.ActivationFunctionType

P = 128
QUADRANT = 32
LANES = 4
WORD = 2
SPANS = LANES // WORD
ALIGN = 64
K_PASS = P * LANES
BANK = 512
BANKS = 8

BATCH = 2
POINTS = 1024
INNER = 512
CHANNELS = 1024
EPS = 1e-5

PASSES = POINTS // K_PASS
ROWS = 2
QBLOCK = ROWS * P
QUARTERS = POINTS // QBLOCK
BLOCKS = BATCH * QUARTERS
HALVES = POINTS // BANK
BLOCKS_PER_HALF = BANK // QBLOCK
CTILES = CHANNELS // P
PAIR = CTILES // QUARTERS
VECTORS = 5

TURN_AHEAD = 1
REGROUP_AHEAD = 2
QUANTISE_AHEAD = 1
PROJECT_LAG = QUARTERS
SHIFT_LAG = PROJECT_LAG - 1
GAIN_STEP = SHIFT_LAG - 2

FLOPS = 2 * BATCH * (POINTS * POINTS * INNER + CHANNELS * INNER * POINTS)


def tile_sgcam_pb_kernel(
    tc, affinity, g_x, w_w_words, w_w_scales, w_b, bn_gamma, bn_beta, bn_mean, bn_var, x, out
):
    nc = tc.nc
    with ExitStack() as ctx:
        keep = ctx.enter_context(tc.tile_pool(name="keep", bufs=1))
        stage = ctx.enter_context(tc.tile_pool(name="stage", bufs=3))
        psum = ctx.enter_context(tc.psum_pool(name="psum", bufs=BANKS))

        identity = keep.tile([P, P], F32, name="identity")
        make_identity(nc, identity[:])
        minus_half = keep.tile([P, CTILES], F32, name="minus_half")
        nc.gpsimd.memset(minus_half[:], -0.5)
        w_scales = keep.tile([P, CHANNELS], U8, name="w_scales", align_bytes=ALIGN)
        nc.vector.memset(w_scales[:].bitcast(I32), 0)
        vector_rows = keep.tile([P, P], BF16, name="vector_rows")
        nc.vector.memset(vector_rows[:], 0.0)
        warm = keep.tile([P, 1], F32, name="warm")
        nc.vector.memset(warm[:], 0.0)
        nc.scalar.activation(out=warm[:], in_=warm[:], func=ACT.Identity)

        for v, vector in enumerate((w_b, bn_gamma, bn_beta, bn_mean, bn_var)):
            nc.scalar.dma_start(
                out=vector_rows[CTILES * v : CTILES * (v + 1), :], in_=vector.rearrange("(i p) -> i p", p=P)
            )
        g_raw = []
        a_raw = []
        x_raw = []
        w_codes = keep.tile([P, CHANNELS], U32, name="w_codes", align_bytes=ALIGN)
        for n in range(BLOCKS + PROJECT_LAG):
            if n < BLOCKS:
                b, quarter = divmod(n, QUARTERS)
                if quarter == 0:
                    g_raw.append(keep.tile([P, PASSES, LANES, INNER], BF16, name="g_raw%d" % b))
                    for g in range(PASSES):
                        nc.sync.dma_start(
                            out=g_raw[b][:, g].rearrange("j (u e) c -> j u (e c)", u=SPANS),
                            in_=g_x[b, g * K_PASS : (g + 1) * K_PASS, :].rearrange(
                                "(u j e) c -> j u (e c)", u=SPANS, e=WORD
                            ),
                        )
                a_raw.append(keep.tile([P, ROWS, POINTS], BF16, name="a_raw%d" % n))
                nc.sync.dma_start(
                    out=a_raw[n][:],
                    in_=affinity[b, quarter * QBLOCK : (quarter + 1) * QBLOCK, :].rearrange(
                        "(p r) s -> p r s", r=ROWS
                    ),
                )
                if b == 0:
                    nc.sync.dma_start(
                        out=w_scales[QUADRANT * quarter : QUADRANT * quarter + LANES, :].bitcast(I32),
                        in_=w_w_scales[0, LANES * quarter : LANES * (quarter + 1), :].bitcast(I32),
                    )
            if n == PROJECT_LAG:
                nc.sync.dma_start(
                    out=w_codes[:].bitcast(I32), in_=w_w_words[0].rearrange("p n t -> p (n t)").bitcast(I32)
                )
            if n >= PROJECT_LAG:
                b, quarter = divmod(n - PROJECT_LAG, QUARTERS)
                x_raw.append(keep.tile([P, PAIR, POINTS], BF16, name="x_raw%d" % (n - PROJECT_LAG)))
                nc.sync.dma_start(
                    out=x_raw[-1][:],
                    in_=x[b, quarter * PAIR * P : (quarter + 1) * PAIR * P, :].rearrange("(i p) q -> p i q", p=P),
                )

        vector_rows_f32 = keep.tile([P, P], F32, name="vector_rows_f32")
        nc.gpsimd.tensor_copy(out=vector_rows_f32[:], in_=vector_rows[:])
        gain = keep.tile([P, CTILES], F32, name="gain")
        shift = keep.tile([P, CTILES], F32, name="shift")

        g_grouped = {}
        g_quantised = {}
        a_grouped = {}
        a_quantised = {}
        y_grouped = {}
        y_quantised = {}
        results = {}

        def regroup_values(b):
            g_grouped[b] = stage.tile([P, PASSES, INNER * LANES], BF16, name="g_grouped", bufs=1, align_bytes=ALIGN)
            for g in range(PASSES):
                nc.vector.tensor_copy(
                    out=g_grouped[b][:, g, :].rearrange("j (l m t) -> j l m t", l=LANES, t=LANES),
                    in_=g_raw[b][:, g].rearrange("j t (m l) -> j l m t", l=LANES),
                )

        def quantise_values(b):
            g_codes = keep.tile([P, PASSES * INNER], U32, name="g_codes%d" % b, align_bytes=ALIGN)
            g_scales = keep.tile([P, PASSES * INNER], U8, name="g_scales%d" % b, align_bytes=ALIGN)
            nc.vector.quantize_mx(
                out=g_codes[:].bitcast(FP8X4), scales=g_scales[:], in_=g_grouped[b][:].rearrange("j g c -> j (g c)")
            )
            g_quantised[b] = (g_codes, g_scales)

        def transpose_block(n):
            words = a_raw[n][:].bitcast(F32)
            a_grouped[n] = stage.tile([P, PASSES, QBLOCK * LANES], BF16, name="a_grouped", align_bytes=ALIGN)
            for g in range(PASSES):
                turned = psum.tile([P, ROWS, SPANS, P], F32, name="turned", tag="bank")
                for r in range(ROWS):
                    for u in range(SPANS):
                        first_word = (g * SPANS + u) * P
                        nc.tensor.transpose(turned[:, r, u, :], words[:, r, first_word : first_word + P], identity[:])
                nc.scalar.copy(
                    out=a_grouped[n][:, g, :].bitcast(F32).rearrange("j (p r u) -> j p r u", r=ROWS, u=SPANS),
                    in_=turned[:].rearrange("j r u p -> j p r u"),
                )

        def quantise_block(n):
            a_codes = stage.tile([P, PASSES * QBLOCK], U32, name="a_codes", align_bytes=ALIGN)
            a_scales = stage.tile([P, PASSES * QBLOCK], U8, name="a_scales", align_bytes=ALIGN)
            nc.vector.quantize_mx(
                out=a_codes[:].bitcast(FP8X4), scales=a_scales[:], in_=a_grouped[n][:].rearrange("j g c -> j (g c)")
            )
            a_quantised[n] = (a_codes, a_scales)

        def first_product(n):
            b, quarter = divmod(n, QUARTERS)
            half, part = divmod(quarter, BLOCKS_PER_HALF)
            a_codes, a_scales = a_quantised[n]
            g_codes, g_scales = g_quantised[b]
            if part == 0:
                y_grouped[b, half] = stage.tile([P, BANK, LANES], BF16, name="y_grouped", align_bytes=ALIGN)
            for sub in range(QBLOCK // P):
                sums = psum.tile([P, LANES, P], F32, name="sums", tag="bank")
                for l in range(LANES):
                    for g in range(PASSES):
                        stationary = slice(g * INNER + l * P, g * INNER + (l + 1) * P)
                        moving = slice(g * QBLOCK + sub * P, g * QBLOCK + (sub + 1) * P)
                        nc.tensor.matmul_mx(
                            out=sums[:, l, :],
                            lhsT=g_codes[:, stationary].bitcast(FP8X4),
                            lhsT_scale=g_scales[:, stationary],
                            rhs=a_codes[:, moving].bitcast(FP8X4),
                            rhs_scale=a_scales[:, moving],
                            start=(g == 0),
                            stop=(g == PASSES - 1),
                        )
                first_point = part * QBLOCK + sub * P
                nc.scalar.copy(
                    out=y_grouped[b, half][:, first_point : first_point + P, :], in_=sums[:].rearrange("m l q -> m q l")
                )
            if part == BLOCKS_PER_HALF - 1:
                y_codes = keep.tile([P, BANK], U32, name="y_codes%d_%d" % (b, half), align_bytes=ALIGN)
                y_scales = keep.tile([P, BANK], U8, name="y_scales%d_%d" % (b, half), align_bytes=ALIGN)
                nc.vector.quantize_mx(
                    out=y_codes[:].bitcast(FP8X4),
                    scales=y_scales[:],
                    in_=y_grouped[b, half][:].rearrange("m q l -> m (q l)"),
                )
                y_quantised[b, half] = (y_codes, y_scales)

        def make_gain_and_shift():
            turned_vectors = psum.tile([P, BANK], F32, name="turned_vectors", tag="bank")
            nc.tensor.transpose(turned_vectors[:, 0:P], vector_rows_f32[:], identity[:])
            per_channel = keep.tile([P, VECTORS, CTILES], F32, name="per_channel")
            nc.scalar.copy(
                out=per_channel[:].rearrange("p v i -> p (v i)"), in_=turned_vectors[:, 0 : VECTORS * CTILES]
            )
            bias_c, gamma_c, beta_c, mean_c, var_c = [per_channel[:, v, :] for v in range(VECTORS)]
            nc.gpsimd.tensor_scalar(out=gain[:], in0=var_c, scalar1=1.0, scalar2=EPS, op0=ALU.mult, op1=ALU.add)
            nc.gpsimd.tensor_tensor(out=gain[:], in0=gain[:], in1=minus_half[:], op=ALU.pow)
            nc.gpsimd.tensor_tensor(out=gain[:], in0=gain[:], in1=gamma_c, op=ALU.mult)
            nc.gpsimd.tensor_tensor(out=shift[:], in0=bias_c, in1=mean_c, op=ALU.subtract)
            nc.gpsimd.tensor_tensor(out=shift[:], in0=shift[:], in1=gain[:], op=ALU.mult)
            nc.gpsimd.tensor_tensor(out=shift[:], in0=shift[:], in1=beta_c, op=ALU.add)

        def add_shift(n):
            b, quarter = divmod(n, QUARTERS)
            even, odd = PAIR * quarter, PAIR * quarter + 1
            results[b, even] = keep.tile([P, POINTS], F32, name="result%d_%d" % (b, even))
            results[b, odd] = keep.tile([P, POINTS], F32, name="result%d_%d" % (b, odd))
            nc.scalar.activation(
                out=results[b, even][:], in_=x_raw[n][:, 0, :], func=ACT.Identity, bias=shift[:, even : even + 1]
            )
            nc.vector.tensor_scalar_add(out=results[b, odd][:], in0=x_raw[n][:, 1, :], scalar1=shift[:, odd : odd + 1])

        def second_product(n):
            b, quarter = divmod(n, QUARTERS)
            for i in (PAIR * quarter, PAIR * quarter + 1):
                channels = slice(i * P, (i + 1) * P)
                for half in range(HALVES):
                    points = slice(half * BANK, (half + 1) * BANK)
                    y_codes, y_scales = y_quantised[b, half]
                    projected = psum.tile([P, BANK], F32, name="projected", tag="bank")
                    nc.tensor.matmul_mx(
                        out=projected[:],
                        lhsT=w_codes[:, channels].bitcast(FP8X4),
                        lhsT_scale=w_scales[:, channels],
                        rhs=y_codes[:].bitcast(FP8X4),
                        rhs_scale=y_scales[:],
                        start=True,
                        stop=True,
                    )
                    nc.vector.scalar_tensor_tensor(
                        out=results[b, i][:, points],
                        in0=projected[:],
                        scalar=gain[:, i : i + 1],
                        in1=results[b, i][:, points],
                        op0=ALU.mult,
                        op1=ALU.add,
                    )
                nc.sync.dma_start(out=out[b, channels, :], in_=results[b, i][:])

        def is_block(n):
            return 0 <= n < BLOCKS

        def later_batch_that_starts(step):
            b, quarter = divmod(step, QUARTERS)
            return b if quarter == 0 and 0 < b < BATCH else None

        regroup_values(0)
        quantise_values(0)
        transpose_block(0)
        for step in range(BLOCKS + PROJECT_LAG):
            if is_block(step + TURN_AHEAD):
                transpose_block(step + TURN_AHEAD)
            if is_block(step):
                quantise_block(step)
            if later_batch_that_starts(step + QUANTISE_AHEAD) is not None:
                quantise_values(later_batch_that_starts(step + QUANTISE_AHEAD))
            if is_block(step):
                first_product(step)
            if later_batch_that_starts(step + REGROUP_AHEAD) is not None:
                regroup_values(later_batch_that_starts(step + REGROUP_AHEAD))
            if step == GAIN_STEP:
                make_gain_and_shift()
            if is_block(step - SHIFT_LAG):
                add_shift(step - SHIFT_LAG)
            if is_block(step - PROJECT_LAG):
                second_product(step - PROJECT_LAG)
